import numpy as np
import ml_dtypes


def mxq(x, axis, fmt="e4m3"):
    dtype, down = {"e4m3": (ml_dtypes.float8_e4m3fn, 7), "e5m2": (ml_dtypes.float8_e5m2, 14)}[fmt]
    v = np.moveaxis(np.asarray(x, np.float32).astype(ml_dtypes.bfloat16).astype(np.float64), axis, -1)
    blocks = v.reshape(v.shape[:-1] + (-1, 32))
    amax = np.abs(blocks).max(-1, keepdims=True)
    byte = np.maximum(np.where(amax > 0, np.frexp(amax)[1] - 1 + 127, 0) - down, 1)
    scale = np.exp2(byte - 127.0)
    codes = (blocks / scale).astype(np.float32).astype(dtype).astype(np.float64)
    return np.moveaxis((codes * scale).reshape(v.shape), -1, axis)


WIDE = False


def mx_kscale(k):
    if not WIDE:
        return np.ones(k)
    levels = np.array([10, -10, 5, -5, 0])
    if k % 512:
        return np.exp2(np.random.permutation(np.resize(levels, k // 32))).repeat(32)
    a = np.empty((k // 512, 16))
    for p in range(k // 512):
        a[p, :8] = np.random.permutation(np.resize(levels, 8))
        for g in range(8):
            far = levels[np.abs(levels - a[p, g]) >= 10]
            a[p, g + 8] = far[np.random.randint(len(far))]
    return np.exp2(a.ravel()).repeat(32)


BF16 = ml_dtypes.bfloat16


def bf(x):
    return np.asarray(x, np.float32).astype(BF16)


def f64(x):
    return np.asarray(x).astype(np.float64)


B, T, D, E, F = 4, 768, 2048, 2048, 8192
EPS = 1e-6


def rms_norm(x, w):
    rms = np.sqrt(np.mean(x * x, axis=-1, keepdims=True) + EPS)
    return x / rms * w


def erf(v):
    a = np.minimum(np.abs(v), 6.0)
    z = 2.0 * a * a
    term = a.copy()
    tot = a.copy()
    for n in range(1, 110):
        term = term * z / (2 * n + 1)
        tot = tot + term
    return np.sign(v) * tot * np.exp(-a * a) * 2.0 / np.sqrt(np.pi)


def gelu_erf(v):
    return 0.5 * v * (1.0 + erf(v / np.sqrt(2.0)))


def setup_inputs():
    s, t = mx_kscale(E), mx_kscale(D)
    return {"attn": bf(np.random.standard_normal((B, T, E)) * 0.6 * s),
            "x": bf(np.random.standard_normal((B, T, D))),
            "wo": bf(np.random.standard_normal((E, D)) / np.sqrt(E) / s[:, None]),
            "bo": bf(np.random.standard_normal(D) * 0.1),
            "mlp_norm_w": bf((1.0 + 0.1 * np.random.standard_normal(D)) * t),
            "w1": bf(np.random.standard_normal((D, F)) / np.sqrt(D) / t[:, None]),
            "b1": bf(np.random.standard_normal(F) * 0.1)}


def reference(attn, x, wo, bo, mlp_norm_w, w1, b1):
    x_mid = f64(x) + (mxq(f64(attn), 2, "e4m3") @ mxq(f64(wo), 0, "e4m3")) + f64(bo)
    h = rms_norm(x_mid, f64(mlp_norm_w))
    g = gelu_erf((mxq(h, 2, "e4m3") @ mxq(f64(w1), 0, "e4m3")) + f64(b1))
    return x_mid, g

@@ -1,0 +1,339 @@
+from contextlib import ExitStack
+
+import concourse.mybir as mybir
+from concourse.masks import make_identity
+
+FLOPS = 2 * 3072 * 2048 * (2048 + 8192)
+
+F32 = mybir.dt.float32
+BF16 = mybir.dt.bfloat16
+U32 = mybir.dt.uint32
+U8 = mybir.dt.uint8
+FP8X4 = mybir.dt.float8_e4m3fn_x4
+ALU = mybir.AluOpType
+ACT = mybir.ActivationFunctionType
+
+P = 128
+NT = 24
+D = 2048
+EPS = 1e-6
+NG = 4
+CW = 512
+N_WO_RAW = 8
+N_RAW = 8 + 32
+XB_ON_GPSIMD = True
+PAIR_READY_SLOT = (4, 8)
+RAW_AHEAD_HEAD = 4
+
+
+def units_in_slot(i):
+    if i < 4:
+        return 0
+    if i < 8:
+        return 1
+    return 2
+
+
+def tile_tinyblock_pb_l_kernel(tc, attn, x, wo, bo, mlp_norm_w, w1, b1, out_0, out_1):
+    nc = tc.nc
+    attn2 = attn.flatten_outer_dims()
+    x2 = x.flatten_outer_dims()
+    o0 = out_0.flatten_outer_dims()
+    o1 = out_1.flatten_outer_dims()
+
+    with ExitStack() as ctx:
+        const = ctx.enter_context(tc.tile_pool(name="const", bufs=1))
+        work = ctx.enter_context(tc.tile_pool(name="work", bufs=2))
+        psum = ctx.enter_context(tc.psum_pool(name="psum", bufs=8))
+
+        def wt(shape, dtype, tag, bufs, idx):
+            return work.tile(shape, dtype, tag=tag, name="%s_%d" % (tag, idx), bufs=bufs, align_bytes=64)
+
+        cnt = {"bank": 0, "lw": 0, "il": 0, "qw": 0, "gst": 0, "grpa": 0}
+
+        def bank():
+            cnt["bank"] += 1
+            return psum.tile([P, 512], F32, tag="bank", name="bank_%d" % cnt["bank"])
+
+        ident = const.tile([P, P], F32, name="ident")
+        neg_half = const.tile([P, 1], F32, name="neg_half")
+        warm = const.tile([P, 1], F32, name="warm")
+        warm2 = const.tile([P, 1], F32, name="warm2")
+        bo_bc = const.tile([P, D], BF16, name="bo_bc")
+        nw_bc = const.tile([P, D], BF16, name="nw_bc")
+        hc = {}
+        hp = {}
+        for j in range(NT):
+            hc[j] = const.tile([P, NG * P], U32, name="hc_%d" % j, align_bytes=64)
+            hp[j] = const.tile([P, P], U8, name="hp_%d" % j, align_bytes=64)
+
+        make_identity(nc, ident[:])
+        ctx.enter_context(tc.manual_schedule())
+
+        araw, xraw, xmid, hbf, ac, ap = {}, {}, {}, {}, {}, {}
+        ss, ms, rstd = {}, {}, {}
+        tpa, tph, grpa, grph = {}, {}, {}, {}
+        raw, grpw, wc, wp, b1bc = {}, {}, {}, {}, {}
+
+        def load_attn(i):
+            if i < NT:
+                araw[i] = wt([P, D], BF16, "araw", 2, i)
+                nc.sync.dma_start(out=araw[i][:], in_=attn2[i * P : (i + 1) * P, :])
+
+        def load_x(i):
+            if i < NT:
+                xraw[i] = wt([P, D], BF16, "xraw", 2, i)
+                nc.sync.dma_start(out=xraw[i][:], in_=x2[i * P : (i + 1) * P, :])
+
+        def load_b1(q):
+            b1bc[q] = wt([P, 2 * CW], BF16, "b1bc", 3, q)
+            nc.sync.dma_start(out=b1bc[q][:], in_=b1[q * 2 * CW : (q + 1) * 2 * CW].partition_broadcast(P))
+
+        def lw_upto(n):
+            while cnt["lw"] < min(n, N_RAW):
+                r = cnt["lw"]
+                g = r % 4
+                if r < N_WO_RAW:
+                    mat, pr = wo, r // 4
+                    raw[r] = wt([P, 4, 2 * CW], BF16, "wcb", 4, 100 + r)
+                else:
+                    mat, pr = w1, r // 4 - 2
+                    raw[r] = wt([P, 4, 2 * CW], BF16, "wraw", 2, r)
+                nc.sync.dma_start(
+                    out=raw[r][:],
+                    in_=mat[g * 512 : (g + 1) * 512, pr * 2 * CW : (pr + 1) * 2 * CW].rearrange("(p j) c -> p j c", j=4),
+                )
+                cnt["lw"] += 1
+
+        def il_upto(n):
+            while cnt["il"] < min(n, 2 * N_RAW):
+                k = cnt["il"]
+                grpw[k] = wt([P, 4 * CW], BF16, "grpw", 3, k)
+                dst = grpw[k][:].rearrange("p (c j) -> p c j", j=4)
+                src = raw[k // 2][:, :, (k % 2) * CW : (k % 2 + 1) * CW].rearrange("p j c -> p c j")
+                if k % 2 == 0 and not (16 <= k < 32):
+                    nc.vector.tensor_copy(out=dst, in_=src)
+                else:
+                    nc.scalar.copy(out=dst, in_=src)
+                cnt["il"] += 1
+
+        def quant_w(k):
+            r = k // 2
+            g = r % 4
+            cid = 2 * (r // 4) + k % 2
+            if g == 0:
+                ab = "a" if (cid // 4) % 2 == 0 else "b"
+                wc[cid] = wt([P, NG * CW], U32, "wc" + ab, 4, cid)
+                wp[cid] = wt([P, CW], U8, "wp" + ab, 4, cid)
+            nc.vector.quantize_mx(
+                out=wc[cid][:, g * CW : (g + 1) * CW].bitcast(FP8X4),
+                scales=wp[cid][4 * g : P, :],
+                in_=grpw[k][:],
+            )
+
+        def tick_q():
+            k = cnt["qw"]
+            if k < 2 * N_RAW:
+                lw_upto(k // 2 + (RAW_AHEAD_HEAD + 1 if k < 2 * N_WO_RAW - 2 * RAW_AHEAD_HEAD else 3))
+                quant_w(k)
+                quant_w(k + 1)
+                cnt["qw"] = k + 2
+
+        def tick_i():
+            il_upto(cnt["qw"] + 2)
+
+        def transposes(src):
+            words = src[:].bitcast(F32)
+            banks = [bank(), bank()]
+            for g in range(NG):
+                for u in range(2):
+                    s = 2 * (g % 2) + u
+                    nc.tensor.transpose(
+                        out=banks[g // 2][:, s * P : (s + 1) * P],
+                        in_=words[:, 256 * g + u : 256 * (g + 1) : 2],
+                        identity=ident[:],
+                    )
+            return banks
+
+        def copy_out(banks):
+            cnt["grpa"] += 1
+            grp = wt([P, D], BF16, "grpa", 2, cnt["grpa"])
+            for b in range(2):
+                nc.scalar.copy(
+                    out=grp[:, b * 1024 : (b + 1) * 1024].bitcast(F32).rearrange("p (g r u) -> p g r u", g=2, u=2),
+                    in_=banks[b][:].rearrange("p (g u r) -> p g r u", g=2, u=2),
+                )
+            return grp
+
+        def quant4(grp, codes, plane):
+            for g in range(NG):
+                nc.vector.quantize_mx(
+                    out=codes[:, g * P : (g + 1) * P].bitcast(FP8X4),
+                    scales=plane[4 * g : P, :],
+                    in_=grp[:, g * 512 : (g + 1) * 512],
+                )
+
+        def mm_pass(acc, lc, lp, cid, g):
+            nc.tensor.matmul_mx(
+                out=acc[:],
+                lhsT=lc[:, g * P : (g + 1) * P].bitcast(FP8X4),
+                lhsT_scale=lp[4 * g : P, :],
+                rhs=wc[cid][:, g * CW : (g + 1) * CW].bitcast(FP8X4),
+                rhs_scale=wp[cid][4 * g : P, :],
+                start=(g == 0),
+                stop=(g == NG - 1),
+            )
+
+        def x_plus_bo(i, pieces):
+            if i < NT:
+                if i not in xmid:
+                    xmid[i] = wt([P, D], F32, "xmid", 2, i)
+                for n in pieces:
+                    sl = slice(n * CW, (n + 1) * CW)
+                    eng = nc.gpsimd if XB_ON_GPSIMD else nc.vector
+                    eng.tensor_tensor(out=xmid[i][:, sl], in0=xraw[i][:, sl], in1=bo_bc[:, sl], op=ALU.add)
+
+        def attn_t(i):
+            if i < NT:
+                tpa[i] = transposes(araw[i])
+
+        def attn_c(i):
+            if i < NT:
+                grpa[i] = copy_out(tpa[i])
+
+        def attn_q(i):
+            if i < NT:
+                ac[i] = wt([P, NG * P], U32, "ac", 3, i)
+                ap[i] = wt([P, P], U8, "ap", 3, i)
+                quant4(grpa[i], ac[i], ap[i])
+
+        def head_extras(t):
+            if t == 0:
+                load_attn(1)
+                nc.sync.dma_start(out=bo_bc[:], in_=bo.partition_broadcast(P))
+                load_x(0)
+            if t == 3:
+                load_x(1)
+                nc.sync.dma_start(out=nw_bc[:], in_=mlp_norm_w.partition_broadcast(P))
+                load_attn(2)
+                load_b1(0)
+            if t == 4:
+                attn_t(1)
+                attn_c(1)
+            if t == 5:
+                attn_q(1)
+
+        def stage1(i):
+            hbf[i] = wt([P, D], BF16, "hbf", 2, i)
+            ss[i] = wt([P, 4], F32, "ss", 2, i)
+            for pr in range(2):
+                accs = [bank(), bank()]
+                for g in range(NG):
+                    if i == 0:
+                        tick_q()
+                        tick_i()
+                        head_extras(4 * pr + g)
+                    for half in range(2):
+                        mm_pass(accs[half], ac[i], ap[i], 2 * pr + half, g)
+                if i == 0:
+                    x_plus_bo(0, (2 * pr, 2 * pr + 1))
+                for half in range(2):
+                    n = 2 * pr + half
+                    sl = slice(n * CW, (n + 1) * CW)
+                    nc.vector.tensor_tensor(out=xmid[i][:, sl], in0=accs[half][:], in1=xmid[i][:, sl], op=ALU.add)
+                x_plus_bo(i + 1, (2 * pr, 2 * pr + 1))
+                for half in range(2):
+                    n = 2 * pr + half
+                    sl = slice(n * CW, (n + 1) * CW)
+                    nc.scalar.activation(
+                        out=hbf[i][:, sl], in_=xmid[i][:, sl], func=ACT.Square, accum_out=ss[i][:, n : n + 1]
+                    )
+            nc.sync.dma_start(out=o0[i * P : (i + 1) * P, :], in_=xmid[i][:])
+            junk = wt([P, 4], F32, "junk", 2, i)
+            ms[i] = wt([P, 1], F32, "ms", 2, i)
+            rstd[i] = wt([P, 1], F32, "rstd", 2, i)
+            nc.scalar.activation(
+                out=junk[:], in_=ss[i][:], func=ACT.Identity, scale=1.0 / D, bias=EPS / 4.0, accum_out=ms[i][:]
+            )
+            nc.gpsimd.tensor_tensor(out=rstd[i][:], in0=ms[i][:], in1=neg_half[:], op=ALU.pow)
+
+        def norm(i):
+            nc.vector.scalar_tensor_tensor(
+                out=hbf[i][:], in0=xmid[i][:], scalar=rstd[i][:, 0:1], in1=nw_bc[:], op0=ALU.mult, op1=ALU.mult
+            )
+
+        def stage2(q, j):
+            accs = [bank(), bank()]
+            for g in range(NG):
+                for half in range(2):
+                    mm_pass(accs[half], hc[j], hp[j], 4 + 2 * q + half, g)
+            cnt["gst"] += 1
+            gst = wt([P, 2 * CW], F32, "gst", 4, cnt["gst"])
+            for half in range(2):
+                sl = slice(half * CW, (half + 1) * CW)
+                nc.vector.tensor_tensor(out=gst[:, sl], in0=accs[half][:], in1=b1bc[q][:, sl], op=ALU.add)
+            nc.scalar.activation(out=gst[:], in_=gst[:], func=ACT.Gelu)
+            nc.sync.dma_start(out=o1[j * P : (j + 1) * P, q * 2 * CW : (q + 1) * 2 * CW], in_=gst[:])
+
+        nc.vector.memset(warm[:], 0.0)
+        nc.vector.memset(neg_half[:], -0.5)
+        nc.scalar.activation(out=warm2[:], in_=warm[:], func=ACT.Gelu)
+        load_attn(0)
+        lw_upto(RAW_AHEAD_HEAD)
+        attn_t(0)
+        attn_c(0)
+        il_upto(2)
+        attn_q(0)
+
+        todo = [(q, j) for j in range(NT) for q in range(2)]
+        done = set()
+        for i in range(NT + 1):
+            load_attn(i + 3)
+            if i > 0:
+                load_x(i + 2)
+            if i < NT:
+                stage1(i)
+            if i == 0:
+                load_x(2)
+            if i == 3:
+                load_b1(1)
+            if i == 20:
+                load_b1(2)
+            ticking = i < 8 or i >= NT - 1
+            if ticking:
+                tick_q()
+            attn_t(i + 2)
+            if i >= 1:
+                tph[i - 1] = transposes(hbf[i - 1])
+            attn_c(i + 2)
+            if i >= 1:
+                grph[i - 1] = copy_out(tph[i - 1])
+            if i < NT:
+                norm(i)
+            if i >= 1:
+                quant4(grph[i - 1], hc[i - 1], hp[i - 1])
+            attn_q(i + 2)
+            if ticking:
+                tick_i()
+            left = units_in_slot(i)
+            for q, j in todo:
+                if left > 0 and (q, j) not in done and j <= i - 2 and i >= PAIR_READY_SLOT[q]:
+                    stage2(q, j)
+                    done.add((q, j))
+                    left -= 1
+            if i == NT:
+                tick_q()
+                tick_i()
+
+        rest = [u for u in todo if u not in done]
+        n0 = len(rest)
+        rest.extend([(q, j) for q in range(2, 8) for j in range(NT)])
+        tick_at = set([0] + [2 + 6 * t for t in range(20)])
+        lb_at = dict([(n0 + 24 * (q - 3) + 1, q) for q in range(3, 8)])
+        for idx, (q, j) in enumerate(rest):
+            stage2(q, j)
+            if idx in tick_at:
+                tick_q()
+                tick_i()
+            if idx in lb_at:
+                load_b1(lb_at[idx])

@@ -21,9 +21,17 @@ NG = 4
 CW = 512
 N_WO_RAW = 8
 N_RAW = 8 + 32
-XB_ON_GPSIMD = True
+XB_GPSIMD_PIECES = ()
 PAIR_READY_SLOT = (4, 8)
 RAW_AHEAD_HEAD = 4
+
+
+def prep_in_slot(i):
+    if i < 8:
+        return 2
+    if i >= NT - 1:
+        return 2
+    return 0
 
 
 def units_in_slot(i):
@@ -61,6 +69,8 @@ def tile_tinyblock_pb_l_kernel(tc, attn, x, wo, bo, mlp_norm_w, w1, b1, out_0, o
         warm2 = const.tile([P, 1], F32, name="warm2")
         bo_bc = const.tile([P, D], BF16, name="bo_bc")
         nw_bc = const.tile([P, D], BF16, name="nw_bc")
+        ident_bf = const.tile([P, P], BF16, name="ident_bf")
+        rows = const.tile([P, 2 * CW], BF16, name="rows")
         hc = {}
         hp = {}
         for j in range(NT):
@@ -68,10 +78,11 @@ def tile_tinyblock_pb_l_kernel(tc, attn, x, wo, bo, mlp_norm_w, w1, b1, out_0, o
             hp[j] = const.tile([P, P], U8, name="hp_%d" % j, align_bytes=64)
 
         make_identity(nc, ident[:])
+        make_identity(nc, ident_bf[:])
         ctx.enter_context(tc.manual_schedule())
 
         araw, xraw, xmid, hbf, ac, ap = {}, {}, {}, {}, {}, {}
-        ss, ms, rstd = {}, {}, {}
+        ss, ms, rstd, s1acc = {}, {}, {}, {}
         tpa, tph, grpa, grph = {}, {}, {}, {}
         raw, grpw, wc, wp, b1bc = {}, {}, {}, {}, {}
 
@@ -87,7 +98,20 @@ def tile_tinyblock_pb_l_kernel(tc, attn, x, wo, bo, mlp_norm_w, w1, b1, out_0, o
 
         def load_b1(q):
             b1bc[q] = wt([P, 2 * CW], BF16, "b1bc", 3, q)
-            nc.sync.dma_start(out=b1bc[q][:], in_=b1[q * 2 * CW : (q + 1) * 2 * CW].partition_broadcast(P))
+            spread(4 + q, b1bc[q][:], nc.scalar.copy)
+
+        def spread(r, dst, eng_copy):
+            cnt["bank"] += 1
+            bk = psum.tile([P, 2 * CW], BF16, tag="bank", name="bank_%d" % cnt["bank"])
+            for s in range(2):
+                nc.tensor.matmul(
+                    out=bk[:, s * CW : (s + 1) * CW],
+                    lhsT=ident_bf[:, r : r + 1].to_broadcast([P, P]),
+                    rhs=rows[:, s * CW : (s + 1) * CW],
+                    start=True,
+                    stop=True,
+                )
+            eng_copy(out=dst, in_=bk[:])
 
         def lw_upto(n):
             while cnt["lw"] < min(n, N_RAW):
@@ -131,28 +155,28 @@ def tile_tinyblock_pb_l_kernel(tc, attn, x, wo, bo, mlp_norm_w, w1, b1, out_0, o
                 in_=grpw[k][:],
             )
 
-        def tick_q():
-            k = cnt["qw"]
-            if k < 2 * N_RAW:
-                lw_upto(k // 2 + (RAW_AHEAD_HEAD + 1 if k < 2 * N_WO_RAW - 2 * RAW_AHEAD_HEAD else 3))
-                quant_w(k)
-                quant_w(k + 1)
-                cnt["qw"] = k + 2
+        def tick_q(n):
+            for t in range(n):
+                k = cnt["qw"]
+                if k < 2 * N_RAW:
+                    lw_upto(k // 2 + (RAW_AHEAD_HEAD + 1 if k < 2 * N_WO_RAW - 2 * RAW_AHEAD_HEAD else 3))
+                    quant_w(k)
+                    cnt["qw"] = k + 1
 
         def tick_i():
             il_upto(cnt["qw"] + 2)
 
-        def transposes(src):
+        def transposes(src, is_sorted):
             words = src[:].bitcast(F32)
             banks = [bank(), bank()]
             for g in range(NG):
                 for u in range(2):
                     s = 2 * (g % 2) + u
-                    nc.tensor.transpose(
-                        out=banks[g // 2][:, s * P : (s + 1) * P],
-                        in_=words[:, 256 * g + u : 256 * (g + 1) : 2],
-                        identity=ident[:],
-                    )
+                    if is_sorted:
+                        in_words = words[:, (2 * g + u) * P : (2 * g + u + 1) * P]
+                    else:
+                        in_words = words[:, 256 * g + u : 256 * (g + 1) : 2]
+                    nc.tensor.transpose(out=banks[g // 2][:, s * P : (s + 1) * P], in_=in_words, identity=ident[:])
             return banks
 
         def copy_out(banks):
@@ -173,11 +197,11 @@ def tile_tinyblock_pb_l_kernel(tc, attn, x, wo, bo, mlp_norm_w, w1, b1, out_0, o
                     in_=grp[:, g * 512 : (g + 1) * 512],
                 )
 
-        def mm_pass(acc, lc, lp, cid, g):
+        def mm_pass(acc, lc, lp_g, cid, g):
             nc.tensor.matmul_mx(
                 out=acc[:],
                 lhsT=lc[:, g * P : (g + 1) * P].bitcast(FP8X4),
-                lhsT_scale=lp[4 * g : P, :],
+                lhsT_scale=lp_g,
                 rhs=wc[cid][:, g * CW : (g + 1) * CW].bitcast(FP8X4),
                 rhs_scale=wp[cid][4 * g : P, :],
                 start=(g == 0),
@@ -189,13 +213,13 @@ def tile_tinyblock_pb_l_kernel(tc, attn, x, wo, bo, mlp_norm_w, w1, b1, out_0, o
                 if i not in xmid:
                     xmid[i] = wt([P, D], F32, "xmid", 2, i)
                 for n in pieces:
-                    sl = slice(n * CW, (n + 1) * CW)
-                    eng = nc.gpsimd if XB_ON_GPSIMD else nc.vector
+                    sl = slice(n * 2 * CW, (n + 1) * 2 * CW)
+                    eng = nc.gpsimd if n in XB_GPSIMD_PIECES else nc.vector
                     eng.tensor_tensor(out=xmid[i][:, sl], in0=xraw[i][:, sl], in1=bo_bc[:, sl], op=ALU.add)
 
         def attn_t(i):
             if i < NT:
-                tpa[i] = transposes(araw[i])
+                tpa[i] = transposes(araw[i], False)
 
         def attn_c(i):
             if i < NT:
@@ -204,24 +228,38 @@ def tile_tinyblock_pb_l_kernel(tc, attn, x, wo, bo, mlp_norm_w, w1, b1, out_0, o
         def attn_q(i):
             if i < NT:
                 ac[i] = wt([P, NG * P], U32, "ac", 3, i)
-                ap[i] = wt([P, P], U8, "ap", 3, i)
-                quant4(grpa[i], ac[i], ap[i])
+                ap[i] = wt([P, NG * P], U8, "ap", 3, i)
+                nc.vector.quantize_mx(out=ac[i][:].bitcast(FP8X4), scales=ap[i][:], in_=grpa[i][:])
 
         def head_extras(t):
-            if t == 0:
+            if t == 2:
                 load_attn(1)
-                nc.sync.dma_start(out=bo_bc[:], in_=bo.partition_broadcast(P))
-                load_x(0)
             if t == 3:
                 load_x(1)
-                nc.sync.dma_start(out=nw_bc[:], in_=mlp_norm_w.partition_broadcast(P))
                 load_attn(2)
-                load_b1(0)
-            if t == 4:
+            if t == 5:
                 attn_t(1)
                 attn_c(1)
-            if t == 5:
+            if t == 6:
+                load_attn(3)
                 attn_q(1)
+                spread(2, nw_bc[:, 0 : 2 * CW], nc.scalar.copy)
+                spread(3, nw_bc[:, 2 * CW : 4 * CW], nc.scalar.copy)
+
+        def stage1_out(i, pr):
+            accs = s1acc[(i, pr)]
+            for half in range(2):
+                n = 2 * pr + half
+                sl = slice(n * CW, (n + 1) * CW)
+                nc.vector.tensor_tensor(out=xmid[i][:, sl], in0=accs[half][:], in1=xmid[i][:, sl], op=ALU.add)
+            if pr == 0:
+                x_plus_bo(i + 1, (0, 1))
+            for half in range(2):
+                n = 2 * pr + half
+                sl = slice(n * CW, (n + 1) * CW)
+                nc.scalar.activation(
+                    out=hbf[i][:, sl], in_=xmid[i][:, sl], func=ACT.Square, accum_out=ss[i][:, n : n + 1]
+                )
 
         def stage1(i):
             hbf[i] = wt([P, D], BF16, "hbf", 2, i)
@@ -230,24 +268,19 @@ def tile_tinyblock_pb_l_kernel(tc, attn, x, wo, bo, mlp_norm_w, w1, b1, out_0, o
                 accs = [bank(), bank()]
                 for g in range(NG):
                     if i == 0:
-                        tick_q()
+                        tick_q(2)
                         tick_i()
                         head_extras(4 * pr + g)
                     for half in range(2):
-                        mm_pass(accs[half], ac[i], ap[i], 2 * pr + half, g)
-                if i == 0:
-                    x_plus_bo(0, (2 * pr, 2 * pr + 1))
-                for half in range(2):
-                    n = 2 * pr + half
-                    sl = slice(n * CW, (n + 1) * CW)
-                    nc.vector.tensor_tensor(out=xmid[i][:, sl], in0=accs[half][:], in1=xmid[i][:, sl], op=ALU.add)
-                x_plus_bo(i + 1, (2 * pr, 2 * pr + 1))
-                for half in range(2):
-                    n = 2 * pr + half
-                    sl = slice(n * CW, (n + 1) * CW)
-                    nc.scalar.activation(
-                        out=hbf[i][:, sl], in_=xmid[i][:, sl], func=ACT.Square, accum_out=ss[i][:, n : n + 1]
-                    )
+                        mm_pass(accs[half], ac[i], ap[i][:, g * P : (g + 1) * P], 2 * pr + half, g)
+                s1acc[(i, pr)] = accs
+                if i > 0:
+                    stage1_out(i, pr)
+            if i == 0:
+                x_plus_bo(0, range(2))
+                load_x(2)
+                stage1_out(0, 0)
+                stage1_out(0, 1)
             nc.sync.dma_start(out=o0[i * P : (i + 1) * P, :], in_=xmid[i][:])
             junk = wt([P, 4], F32, "junk", 2, i)
             ms[i] = wt([P, 1], F32, "ms", 2, i)
@@ -258,28 +291,48 @@ def tile_tinyblock_pb_l_kernel(tc, attn, x, wo, bo, mlp_norm_w, w1, b1, out_0, o
             nc.gpsimd.tensor_tensor(out=rstd[i][:], in0=ms[i][:], in1=neg_half[:], op=ALU.pow)
 
         def norm(i):
-            nc.vector.scalar_tensor_tensor(
-                out=hbf[i][:], in0=xmid[i][:], scalar=rstd[i][:, 0:1], in1=nw_bc[:], op0=ALU.mult, op1=ALU.mult
-            )
+            for g in range(NG):
+                gs = slice(g * 512, (g + 1) * 512)
+                for u in range(2):
+                    nc.vector.scalar_tensor_tensor(
+                        out=hbf[i][:, (2 * g + u) * 256 : (2 * g + u + 1) * 256].rearrange("p (m e) -> p m e", e=2),
+                        in0=xmid[i][:, gs].rearrange("p (m u e) -> p u m e", u=2, e=2)[:, u, :, :],
+                        scalar=rstd[i][:, 0:1],
+                        in1=nw_bc[:, gs].rearrange("p (m u e) -> p u m e", u=2, e=2)[:, u, :, :],
+                        op0=ALU.mult,
+                        op1=ALU.mult,
+                    )
 
         def stage2(q, j):
             accs = [bank(), bank()]
             for g in range(NG):
                 for half in range(2):
-                    mm_pass(accs[half], hc[j], hp[j], 4 + 2 * q + half, g)
+                    mm_pass(accs[half], hc[j], hp[j][4 * g : P, :], 4 + 2 * q + half, g)
             cnt["gst"] += 1
             gst = wt([P, 2 * CW], F32, "gst", 4, cnt["gst"])
             for half in range(2):
                 sl = slice(half * CW, (half + 1) * CW)
                 nc.vector.tensor_tensor(out=gst[:, sl], in0=accs[half][:], in1=b1bc[q][:, sl], op=ALU.add)
-            nc.scalar.activation(out=gst[:], in_=gst[:], func=ACT.Gelu)
-            nc.sync.dma_start(out=o1[j * P : (j + 1) * P, q * 2 * CW : (q + 1) * 2 * CW], in_=gst[:])
+            parts = 2 if (q, j) == (7, NT - 1) else 1
+            w = 2 * CW // parts
+            for s in range(parts):
+                nc.scalar.activation(out=gst[:, s * w : (s + 1) * w], in_=gst[:, s * w : (s + 1) * w], func=ACT.Gelu)
+                nc.sync.dma_start(
+                    out=o1[j * P : (j + 1) * P, q * 2 * CW + s * w : q * 2 * CW + (s + 1) * w], in_=gst[:, s * w : (s + 1) * w]
+                )
 
         nc.vector.memset(warm[:], 0.0)
         nc.vector.memset(neg_half[:], -0.5)
         nc.scalar.activation(out=warm2[:], in_=warm[:], func=ACT.Gelu)
+        nc.vector.memset(rows[:], 0.0)
         load_attn(0)
+        nc.sync.dma_start(out=rows[0:2, :], in_=bo.rearrange("(r c) -> r c", c=2 * CW))
+        nc.sync.dma_start(out=rows[2:4, :], in_=mlp_norm_w.rearrange("(r c) -> r c", c=2 * CW))
+        nc.sync.dma_start(out=rows[4:12, :], in_=b1.rearrange("(r c) -> r c", c=2 * CW))
         lw_upto(RAW_AHEAD_HEAD)
+        load_x(0)
+        spread(0, bo_bc[:, 0 : 2 * CW], nc.vector.tensor_copy)
+        spread(1, bo_bc[:, 2 * CW : 4 * CW], nc.vector.tensor_copy)
         attn_t(0)
         attn_c(0)
         il_upto(2)
@@ -288,23 +341,21 @@ def tile_tinyblock_pb_l_kernel(tc, attn, x, wo, bo, mlp_norm_w, w1, b1, out_0, o
         todo = [(q, j) for j in range(NT) for q in range(2)]
         done = set()
         for i in range(NT + 1):
-            load_attn(i + 3)
             if i > 0:
+                load_attn(i + 3)
                 load_x(i + 2)
             if i < NT:
                 stage1(i)
-            if i == 0:
-                load_x(2)
-            if i == 3:
+            if i == 5:
                 load_b1(1)
+            if i == 1:
+                load_b1(0)
             if i == 20:
                 load_b1(2)
-            ticking = i < 8 or i >= NT - 1
-            if ticking:
-                tick_q()
+            tick_q(prep_in_slot(i))
             attn_t(i + 2)
             if i >= 1:
-                tph[i - 1] = transposes(hbf[i - 1])
+                tph[i - 1] = transposes(hbf[i - 1], True)
             attn_c(i + 2)
             if i >= 1:
                 grph[i - 1] = copy_out(tph[i - 1])
@@ -313,8 +364,7 @@ def tile_tinyblock_pb_l_kernel(tc, attn, x, wo, bo, mlp_norm_w, w1, b1, out_0, o
             if i >= 1:
                 quant4(grph[i - 1], hc[i - 1], hp[i - 1])
             attn_q(i + 2)
-            if ticking:
-                tick_i()
+            tick_i()
             left = units_in_slot(i)
             for q, j in todo:
                 if left > 0 and (q, j) not in done and j <= i - 2 and i >= PAIR_READY_SLOT[q]:
@@ -322,7 +372,7 @@ def tile_tinyblock_pb_l_kernel(tc, attn, x, wo, bo, mlp_norm_w, w1, b1, out_0, o
                     done.add((q, j))
                     left -= 1
             if i == NT:
-                tick_q()
+                tick_q(2)
                 tick_i()
 
         rest = [u for u in todo if u not in done]
@@ -333,7 +383,7 @@ def tile_tinyblock_pb_l_kernel(tc, attn, x, wo, bo, mlp_norm_w, w1, b1, out_0, o
         for idx, (q, j) in enumerate(rest):
             stage2(q, j)
             if idx in tick_at:
-                tick_q()
+                tick_q(2)
                 tick_i()
             if idx in lb_at:
                 load_b1(lb_at[idx])

@@ -21,9 +21,13 @@ NG = 4
 CW = 512
 N_WO_RAW = 8
 N_RAW = 8 + 32
-XB_GPSIMD_PIECES = ()
+XB_GPSIMD_PIECES = (0, 1)
 PAIR_READY_SLOT = (4, 8)
 RAW_AHEAD_HEAD = 4
+STAGE_TAGS = (
+    ("gst", 4), ("araw", 2), ("gst", 4), ("xraw", 2), ("gst", 4), ("hbf", 2),
+    ("gst", 4), ("grpa", 2), ("araw", 2), ("xraw", 2), ("hbf", 2), ("grpa", 2),
+)
 
 
 def prep_in_slot(i):
@@ -57,7 +61,7 @@ def tile_tinyblock_pb_l_kernel(tc, attn, x, wo, bo, mlp_norm_w, w1, b1, out_0, o
         def wt(shape, dtype, tag, bufs, idx):
             return work.tile(shape, dtype, tag=tag, name="%s_%d" % (tag, idx), bufs=bufs, align_bytes=64)
 
-        cnt = {"bank": 0, "lw": 0, "il": 0, "qw": 0, "gst": 0, "grpa": 0}
+        cnt = {"bank": 0, "lw": 0, "il": 0, "qw": 0, "gst": 0, "grpa": 0, "phase2": 0}
 
         def bank():
             cnt["bank"] += 1
@@ -246,14 +250,21 @@ def tile_tinyblock_pb_l_kernel(tc, attn, x, wo, bo, mlp_norm_w, w1, b1, out_0, o
                 spread(2, nw_bc[:, 0 : 2 * CW], nc.scalar.copy)
                 spread(3, nw_bc[:, 2 * CW : 4 * CW], nc.scalar.copy)
 
+        def mid_slot(i):
+            if i >= 2:
+                quant4(grph[i - 2], hc[i - 2], hp[i - 2])
+            if i >= 1:
+                attn_q(i + 1)
+            tick_q(prep_in_slot(i))
+
         def stage1_out(i, pr):
             accs = s1acc[(i, pr)]
             for half in range(2):
                 n = 2 * pr + half
                 sl = slice(n * CW, (n + 1) * CW)
                 nc.vector.tensor_tensor(out=xmid[i][:, sl], in0=accs[half][:], in1=xmid[i][:, sl], op=ALU.add)
-            if pr == 0:
-                x_plus_bo(i + 1, (0, 1))
+            if pr == 1:
+                mid_slot(i)
             for half in range(2):
                 n = 2 * pr + half
                 sl = slice(n * CW, (n + 1) * CW)
@@ -278,6 +289,7 @@ def tile_tinyblock_pb_l_kernel(tc, attn, x, wo, bo, mlp_norm_w, w1, b1, out_0, o
                     stage1_out(i, pr)
             if i == 0:
                 x_plus_bo(0, range(2))
+                x_plus_bo(1, range(2))
                 load_x(2)
                 stage1_out(0, 0)
                 stage1_out(0, 1)
@@ -289,6 +301,7 @@ def tile_tinyblock_pb_l_kernel(tc, attn, x, wo, bo, mlp_norm_w, w1, b1, out_0, o
                 out=junk[:], in_=ss[i][:], func=ACT.Identity, scale=1.0 / D, bias=EPS / 4.0, accum_out=ms[i][:]
             )
             nc.gpsimd.tensor_tensor(out=rstd[i][:], in0=ms[i][:], in1=neg_half[:], op=ALU.pow)
+            x_plus_bo(i + 2, (0, 1))
 
         def norm(i):
             for g in range(NG):
@@ -309,7 +322,10 @@ def tile_tinyblock_pb_l_kernel(tc, attn, x, wo, bo, mlp_norm_w, w1, b1, out_0, o
                 for half in range(2):
                     mm_pass(accs[half], hc[j], hp[j][4 * g : P, :], 4 + 2 * q + half, g)
             cnt["gst"] += 1
-            gst = wt([P, 2 * CW], F32, "gst", 4, cnt["gst"])
+            tag, bufs = "gst", 4
+            if cnt["phase2"] > 0:
+                tag, bufs = STAGE_TAGS[cnt["gst"] % len(STAGE_TAGS)]
+            gst = wt([P, 2 * CW], F32, tag, bufs, 1000 + cnt["gst"])
             for half in range(2):
                 sl = slice(half * CW, (half + 1) * CW)
                 nc.vector.tensor_tensor(out=gst[:, sl], in0=accs[half][:], in1=b1bc[q][:, sl], op=ALU.add)
@@ -340,7 +356,7 @@ def tile_tinyblock_pb_l_kernel(tc, attn, x, wo, bo, mlp_norm_w, w1, b1, out_0, o
 
         todo = [(q, j) for j in range(NT) for q in range(2)]
         done = set()
-        for i in range(NT + 1):
+        for i in range(NT + 2):
             if i > 0:
                 load_attn(i + 3)
                 load_x(i + 2)
@@ -352,18 +368,16 @@ def tile_tinyblock_pb_l_kernel(tc, attn, x, wo, bo, mlp_norm_w, w1, b1, out_0, o
                 load_b1(0)
             if i == 20:
                 load_b1(2)
-            tick_q(prep_in_slot(i))
+            if i >= NT:
+                mid_slot(i)
             attn_t(i + 2)
-            if i >= 1:
+            if 1 <= i <= NT:
                 tph[i - 1] = transposes(hbf[i - 1], True)
             attn_c(i + 2)
-            if i >= 1:
+            if 1 <= i <= NT:
                 grph[i - 1] = copy_out(tph[i - 1])
             if i < NT:
                 norm(i)
-            if i >= 1:
-                quant4(grph[i - 1], hc[i - 1], hp[i - 1])
-            attn_q(i + 2)
             tick_i()
             left = units_in_slot(i)
             for q, j in todo:
@@ -371,10 +385,8 @@ def tile_tinyblock_pb_l_kernel(tc, attn, x, wo, bo, mlp_norm_w, w1, b1, out_0, o
                     stage2(q, j)
                     done.add((q, j))
                     left -= 1
-            if i == NT:
-                tick_q(2)
-                tick_i()
 
+        cnt["phase2"] = 1
         rest = [u for u in todo if u not in done]
         n0 = len(rest)
         rest.extend([(q, j) for q in range(2, 8) for j in range(NT)])

@@ -22,6 +22,9 @@ CW = 512
 N_WO_RAW = 8
 N_RAW = 8 + 32
 XB_GPSIMD_PIECES = (0, 1)
+G2_FROM = 10
+SORT_FROM = 12
+IL_ALL_VECTOR_FROM = 40
 PAIR_READY_SLOT = (4, 8)
 RAW_AHEAD_HEAD = 4
 STAGE_TAGS = (
@@ -87,8 +90,9 @@ def tile_tinyblock_pb_l_kernel(tc, attn, x, wo, bo, mlp_norm_w, w1, b1, out_0, o
 
         araw, xraw, xmid, hbf, ac, ap = {}, {}, {}, {}, {}, {}
         ss, ms, rstd, s1acc = {}, {}, {}, {}
-        tpa, tph, grpa, grph = {}, {}, {}, {}
+        tpa, tph, grpa, grph, asort = {}, {}, {}, {}, {}
         raw, grpw, wc, wp, b1bc = {}, {}, {}, {}, {}
+        held = {"unit": None}
 
         def load_attn(i):
             if i < NT:
@@ -136,10 +140,14 @@ def tile_tinyblock_pb_l_kernel(tc, attn, x, wo, bo, mlp_norm_w, w1, b1, out_0, o
         def il_upto(n):
             while cnt["il"] < min(n, 2 * N_RAW):
                 k = cnt["il"]
-                grpw[k] = wt([P, 4 * CW], BF16, "grpw", 3, k)
+                on_vector = k % 2 == 0 or k >= IL_ALL_VECTOR_FROM
+                if k % 2 == 0:
+                    grpw[k] = wt([P, 4 * CW], BF16, "grpv", 1, k)
+                else:
+                    grpw[k] = wt([P, 4 * CW], BF16, "grps", 2, k)
                 dst = grpw[k][:].rearrange("p (c j) -> p c j", j=4)
                 src = raw[k // 2][:, :, (k % 2) * CW : (k % 2 + 1) * CW].rearrange("p j c -> p c j")
-                if k % 2 == 0 and not (16 <= k < 32):
+                if on_vector:
                     nc.vector.tensor_copy(out=dst, in_=src)
                 else:
                     nc.scalar.copy(out=dst, in_=src)
@@ -218,11 +226,21 @@ def tile_tinyblock_pb_l_kernel(tc, attn, x, wo, bo, mlp_norm_w, w1, b1, out_0, o
                     xmid[i] = wt([P, D], F32, "xmid", 2, i)
                 for n in pieces:
                     sl = slice(n * 2 * CW, (n + 1) * 2 * CW)
-                    eng = nc.gpsimd if n in XB_GPSIMD_PIECES else nc.vector
+                    eng = nc.vector if (n == 1 and 2 <= i < G2_FROM) else nc.gpsimd
                     eng.tensor_tensor(out=xmid[i][:, sl], in0=xraw[i][:, sl], in1=bo_bc[:, sl], op=ALU.add)
 
+        def attn_sort(i):
+            if SORT_FROM <= i < NT:
+                asort[i] = wt([P, D], BF16, "gst", 4, 2000 + i)
+                nc.scalar.copy(
+                    out=asort[i][:].bitcast(F32).rearrange("p (g u m) -> p g u m", g=NG, u=2),
+                    in_=araw[i][:].bitcast(F32).rearrange("p (g m u) -> p g u m", g=NG, u=2),
+                )
+
         def attn_t(i):
-            if i < NT:
+            if SORT_FROM <= i < NT:
+                tpa[i] = transposes(asort[i], True)
+            elif i < NT:
                 tpa[i] = transposes(araw[i], False)
 
         def attn_c(i):
@@ -231,8 +249,8 @@ def tile_tinyblock_pb_l_kernel(tc, attn, x, wo, bo, mlp_norm_w, w1, b1, out_0, o
 
         def attn_q(i):
             if i < NT:
-                ac[i] = wt([P, NG * P], U32, "ac", 3, i)
-                ap[i] = wt([P, NG * P], U8, "ap", 3, i)
+                ac[i] = wt([P, NG * P], U32, "ac", 2, i)
+                ap[i] = wt([P, NG * P], U8, "ap", 2, i)
                 nc.vector.quantize_mx(out=ac[i][:].bitcast(FP8X4), scales=ap[i][:], in_=grpa[i][:])
 
         def head_extras(t):
@@ -256,6 +274,8 @@ def tile_tinyblock_pb_l_kernel(tc, attn, x, wo, bo, mlp_norm_w, w1, b1, out_0, o
             if i >= 1:
                 attn_q(i + 1)
             tick_q(prep_in_slot(i))
+            if 2 <= i + 1 < G2_FROM:
+                x_plus_bo(i + 1, (1,))
 
         def stage1_out(i, pr):
             accs = s1acc[(i, pr)]
@@ -301,7 +321,7 @@ def tile_tinyblock_pb_l_kernel(tc, attn, x, wo, bo, mlp_norm_w, w1, b1, out_0, o
                 out=junk[:], in_=ss[i][:], func=ACT.Identity, scale=1.0 / D, bias=EPS / 4.0, accum_out=ms[i][:]
             )
             nc.gpsimd.tensor_tensor(out=rstd[i][:], in0=ms[i][:], in1=neg_half[:], op=ALU.pow)
-            x_plus_bo(i + 2, (0, 1))
+            x_plus_bo(i + 2, (0, 1) if i + 2 >= G2_FROM else (0,))
 
         def norm(i):
             for g in range(NG):
@@ -326,16 +346,31 @@ def tile_tinyblock_pb_l_kernel(tc, attn, x, wo, bo, mlp_norm_w, w1, b1, out_0, o
             if cnt["phase2"] > 0:
                 tag, bufs = STAGE_TAGS[cnt["gst"] % len(STAGE_TAGS)]
             gst = wt([P, 2 * CW], F32, tag, bufs, 1000 + cnt["gst"])
-            for half in range(2):
-                sl = slice(half * CW, (half + 1) * CW)
-                nc.vector.tensor_tensor(out=gst[:, sl], in0=accs[half][:], in1=b1bc[q][:, sl], op=ALU.add)
-            parts = 2 if (q, j) == (7, NT - 1) else 1
-            w = 2 * CW // parts
-            for s in range(parts):
-                nc.scalar.activation(out=gst[:, s * w : (s + 1) * w], in_=gst[:, s * w : (s + 1) * w], func=ACT.Gelu)
-                nc.sync.dma_start(
-                    out=o1[j * P : (j + 1) * P, q * 2 * CW + s * w : q * 2 * CW + (s + 1) * w], in_=gst[:, s * w : (s + 1) * w]
-                )
+            lo, hi = slice(0, CW), slice(CW, 2 * CW)
+            nc.vector.tensor_tensor(out=gst[:, lo], in0=accs[0][:], in1=b1bc[q][:, lo], op=ALU.add)
+            if cnt["phase2"] > 0 and (q, j) != (7, NT - 1):
+                nc.scalar.copy(out=gst[:, hi], in_=accs[1][:])
+                nc.vector.tensor_tensor(out=gst[:, hi], in0=gst[:, hi], in1=b1bc[q][:, hi], op=ALU.add)
+                finish_unit()
+                held["unit"] = (gst, q, j)
+            else:
+                nc.vector.tensor_tensor(out=gst[:, hi], in0=accs[1][:], in1=b1bc[q][:, hi], op=ALU.add)
+                finish_unit()
+                held["unit"] = (gst, q, j)
+                finish_unit()
+
+        def finish_unit():
+            if held["unit"] is not None:
+                gst, q, j = held["unit"]
+                held["unit"] = None
+                parts = 2 if (q, j) == (7, NT - 1) else 1
+                w = 2 * CW // parts
+                for s in range(parts):
+                    nc.scalar.activation(out=gst[:, s * w : (s + 1) * w], in_=gst[:, s * w : (s + 1) * w], func=ACT.Gelu)
+                    nc.sync.dma_start(
+                        out=o1[j * P : (j + 1) * P, q * 2 * CW + s * w : q * 2 * CW + (s + 1) * w],
+                        in_=gst[:, s * w : (s + 1) * w],
+                    )
 
         nc.vector.memset(warm[:], 0.0)
         nc.vector.memset(neg_half[:], -0.5)
@@ -360,6 +395,7 @@ def tile_tinyblock_pb_l_kernel(tc, attn, x, wo, bo, mlp_norm_w, w1, b1, out_0, o
             if i > 0:
                 load_attn(i + 3)
                 load_x(i + 2)
+            attn_sort(i + 2)
             if i < NT:
                 stage1(i)
             if i == 5:
@@ -399,3 +435,4 @@ def tile_tinyblock_pb_l_kernel(tc, attn, x, wo, bo, mlp_norm_w, w1, b1, out_0, o
                 tick_i()
             if idx in lb_at:
                 load_b1(lb_at[idx])
+        finish_unit()

@@ -22,9 +22,6 @@ CW = 512
 N_WO_RAW = 8
 N_RAW = 8 + 32
 XB_GPSIMD_PIECES = (0, 1)
-G2_FROM = 10
-SORT_FROM = 12
-IL_ALL_VECTOR_FROM = 40
 PAIR_READY_SLOT = (4, 8)
 RAW_AHEAD_HEAD = 4
 STAGE_TAGS = (
@@ -90,9 +87,8 @@ def tile_tinyblock_pb_l_kernel(tc, attn, x, wo, bo, mlp_norm_w, w1, b1, out_0, o
 
         araw, xraw, xmid, hbf, ac, ap = {}, {}, {}, {}, {}, {}
         ss, ms, rstd, s1acc = {}, {}, {}, {}
-        tpa, tph, grpa, grph, asort = {}, {}, {}, {}, {}
+        tpa, tph, grpa, grph = {}, {}, {}, {}
         raw, grpw, wc, wp, b1bc = {}, {}, {}, {}, {}
-        held = {"unit": None}
 
         def load_attn(i):
             if i < NT:
@@ -140,14 +136,10 @@ def tile_tinyblock_pb_l_kernel(tc, attn, x, wo, bo, mlp_norm_w, w1, b1, out_0, o
         def il_upto(n):
             while cnt["il"] < min(n, 2 * N_RAW):
                 k = cnt["il"]
-                on_vector = k % 2 == 0 or k >= IL_ALL_VECTOR_FROM
-                if k % 2 == 0:
-                    grpw[k] = wt([P, 4 * CW], BF16, "grpv", 1, k)
-                else:
-                    grpw[k] = wt([P, 4 * CW], BF16, "grps", 2, k)
+                grpw[k] = wt([P, 4 * CW], BF16, "grpw", 3, k)
                 dst = grpw[k][:].rearrange("p (c j) -> p c j", j=4)
                 src = raw[k // 2][:, :, (k % 2) * CW : (k % 2 + 1) * CW].rearrange("p j c -> p c j")
-                if on_vector:
+                if k % 2 == 0 and not (16 <= k < 32):
                     nc.vector.tensor_copy(out=dst, in_=src)
                 else:
                     nc.scalar.copy(out=dst, in_=src)
@@ -226,21 +218,11 @@ def tile_tinyblock_pb_l_kernel(tc, attn, x, wo, bo, mlp_norm_w, w1, b1, out_0, o
                     xmid[i] = wt([P, D], F32, "xmid", 2, i)
                 for n in pieces:
                     sl = slice(n * 2 * CW, (n + 1) * 2 * CW)
-                    eng = nc.vector if (n == 1 and 2 <= i < G2_FROM) else nc.gpsimd
+                    eng = nc.gpsimd if n in XB_GPSIMD_PIECES else nc.vector
                     eng.tensor_tensor(out=xmid[i][:, sl], in0=xraw[i][:, sl], in1=bo_bc[:, sl], op=ALU.add)
 
-        def attn_sort(i):
-            if SORT_FROM <= i < NT:
-                asort[i] = wt([P, D], BF16, "gst", 4, 2000 + i)
-                nc.scalar.copy(
-                    out=asort[i][:].bitcast(F32).rearrange("p (g u m) -> p g u m", g=NG, u=2),
-                    in_=araw[i][:].bitcast(F32).rearrange("p (g m u) -> p g u m", g=NG, u=2),
-                )
-
         def attn_t(i):
-            if SORT_FROM <= i < NT:
-                tpa[i] = transposes(asort[i], True)
-            elif i < NT:
+            if i < NT:
                 tpa[i] = transposes(araw[i], False)
 
         def attn_c(i):
@@ -249,8 +231,8 @@ def tile_tinyblock_pb_l_kernel(tc, attn, x, wo, bo, mlp_norm_w, w1, b1, out_0, o
 
         def attn_q(i):
             if i < NT:
-                ac[i] = wt([P, NG * P], U32, "ac", 2, i)
-                ap[i] = wt([P, NG * P], U8, "ap", 2, i)
+                ac[i] = wt([P, NG * P], U32, "ac", 3, i)
+                ap[i] = wt([P, NG * P], U8, "ap", 3, i)
                 nc.vector.quantize_mx(out=ac[i][:].bitcast(FP8X4), scales=ap[i][:], in_=grpa[i][:])
 
         def head_extras(t):
@@ -274,8 +256,6 @@ def tile_tinyblock_pb_l_kernel(tc, attn, x, wo, bo, mlp_norm_w, w1, b1, out_0, o
             if i >= 1:
                 attn_q(i + 1)
             tick_q(prep_in_slot(i))
-            if 2 <= i + 1 < G2_FROM:
-                x_plus_bo(i + 1, (1,))
 
         def stage1_out(i, pr):
             accs = s1acc[(i, pr)]
@@ -297,13 +277,17 @@ def tile_tinyblock_pb_l_kernel(tc, attn, x, wo, bo, mlp_norm_w, w1, b1, out_0, o
             ss[i] = wt([P, 4], F32, "ss", 2, i)
             for pr in range(2):
                 accs = [bank(), bank()]
-                for g in range(NG):
-                    if i == 0:
+                if i == 0:
+                    for g in range(NG):
                         tick_q(2)
                         tick_i()
                         head_extras(4 * pr + g)
+                        for half in range(2):
+                            mm_pass(accs[half], ac[i], ap[i][:, g * P : (g + 1) * P], 2 * pr + half, g)
+                else:
                     for half in range(2):
-                        mm_pass(accs[half], ac[i], ap[i][:, g * P : (g + 1) * P], 2 * pr + half, g)
+                        for g in range(NG):
+                            mm_pass(accs[half], ac[i], ap[i][:, g * P : (g + 1) * P], 2 * pr + half, g)
                 s1acc[(i, pr)] = accs
                 if i > 0:
                     stage1_out(i, pr)
@@ -321,7 +305,7 @@ def tile_tinyblock_pb_l_kernel(tc, attn, x, wo, bo, mlp_norm_w, w1, b1, out_0, o
                 out=junk[:], in_=ss[i][:], func=ACT.Identity, scale=1.0 / D, bias=EPS / 4.0, accum_out=ms[i][:]
             )
             nc.gpsimd.tensor_tensor(out=rstd[i][:], in0=ms[i][:], in1=neg_half[:], op=ALU.pow)
-            x_plus_bo(i + 2, (0, 1) if i + 2 >= G2_FROM else (0,))
+            x_plus_bo(i + 2, (0, 1))
 
         def norm(i):
             for g in range(NG):
@@ -338,39 +322,24 @@ def tile_tinyblock_pb_l_kernel(tc, attn, x, wo, bo, mlp_norm_w, w1, b1, out_0, o
 
         def stage2(q, j):
             accs = [bank(), bank()]
-            for g in range(NG):
-                for half in range(2):
+            for half in range(2):
+                for g in range(NG):
                     mm_pass(accs[half], hc[j], hp[j][4 * g : P, :], 4 + 2 * q + half, g)
             cnt["gst"] += 1
             tag, bufs = "gst", 4
             if cnt["phase2"] > 0:
                 tag, bufs = STAGE_TAGS[cnt["gst"] % len(STAGE_TAGS)]
             gst = wt([P, 2 * CW], F32, tag, bufs, 1000 + cnt["gst"])
-            lo, hi = slice(0, CW), slice(CW, 2 * CW)
-            nc.vector.tensor_tensor(out=gst[:, lo], in0=accs[0][:], in1=b1bc[q][:, lo], op=ALU.add)
-            if cnt["phase2"] > 0 and (q, j) != (7, NT - 1):
-                nc.scalar.copy(out=gst[:, hi], in_=accs[1][:])
-                nc.vector.tensor_tensor(out=gst[:, hi], in0=gst[:, hi], in1=b1bc[q][:, hi], op=ALU.add)
-                finish_unit()
-                held["unit"] = (gst, q, j)
-            else:
-                nc.vector.tensor_tensor(out=gst[:, hi], in0=accs[1][:], in1=b1bc[q][:, hi], op=ALU.add)
-                finish_unit()
-                held["unit"] = (gst, q, j)
-                finish_unit()
-
-        def finish_unit():
-            if held["unit"] is not None:
-                gst, q, j = held["unit"]
-                held["unit"] = None
-                parts = 2 if (q, j) == (7, NT - 1) else 1
-                w = 2 * CW // parts
-                for s in range(parts):
-                    nc.scalar.activation(out=gst[:, s * w : (s + 1) * w], in_=gst[:, s * w : (s + 1) * w], func=ACT.Gelu)
-                    nc.sync.dma_start(
-                        out=o1[j * P : (j + 1) * P, q * 2 * CW + s * w : q * 2 * CW + (s + 1) * w],
-                        in_=gst[:, s * w : (s + 1) * w],
-                    )
+            for half in range(2):
+                sl = slice(half * CW, (half + 1) * CW)
+                nc.vector.tensor_tensor(out=gst[:, sl], in0=accs[half][:], in1=b1bc[q][:, sl], op=ALU.add)
+            parts = 2 if (q, j) == (7, NT - 1) else 1
+            w = 2 * CW // parts
+            for s in range(parts):
+                nc.scalar.activation(out=gst[:, s * w : (s + 1) * w], in_=gst[:, s * w : (s + 1) * w], func=ACT.Gelu)
+                nc.sync.dma_start(
+                    out=o1[j * P : (j + 1) * P, q * 2 * CW + s * w : q * 2 * CW + (s + 1) * w], in_=gst[:, s * w : (s + 1) * w]
+                )
 
         nc.vector.memset(warm[:], 0.0)
         nc.vector.memset(neg_half[:], -0.5)
@@ -395,7 +364,6 @@ def tile_tinyblock_pb_l_kernel(tc, attn, x, wo, bo, mlp_norm_w, w1, b1, out_0, o
             if i > 0:
                 load_attn(i + 3)
                 load_x(i + 2)
-            attn_sort(i + 2)
             if i < NT:
                 stage1(i)
             if i == 5:
@@ -435,4 +403,3 @@ def tile_tinyblock_pb_l_kernel(tc, attn, x, wo, bo, mlp_norm_w, w1, b1, out_0, o
                 tick_i()
             if idx in lb_at:
                 load_b1(lb_at[idx])
-        finish_unit()

from contextlib import ExitStack

import concourse.mybir as mybir
from concourse.masks import make_identity

FLOPS = 2 * 3072 * 2048 * (2048 + 8192)

F32 = mybir.dt.float32
BF16 = mybir.dt.bfloat16
U32 = mybir.dt.uint32
U8 = mybir.dt.uint8
FP8X4 = mybir.dt.float8_e4m3fn_x4
ALU = mybir.AluOpType
ACT = mybir.ActivationFunctionType

P = 128
NT = 24
D = 2048
EPS = 1e-6
NG = 4
CW = 512
N_WO_RAW = 8
N_RAW = 8 + 32
XB_GPSIMD_PIECES = (0, 1)
PAIR_READY_SLOT = (4, 8)
RAW_AHEAD_HEAD = 4
STAGE_TAGS = (
    ("gst", 4), ("araw", 2), ("gst", 4), ("xraw", 2), ("gst", 4), ("hbf", 2),
    ("gst", 4), ("grpa", 2), ("araw", 2), ("xraw", 2), ("hbf", 2), ("grpa", 2),
)


def prep_in_slot(i):
    if i < 8:
        return 2
    if i >= NT - 1:
        return 2
    return 0


def units_in_slot(i):
    if i < 4:
        return 0
    if i < 8:
        return 1
    return 2


def tile_tinyblock_pb_l_kernel(tc, attn, x, wo, bo, mlp_norm_w, w1, b1, out_0, out_1):
    nc = tc.nc
    attn2 = attn.flatten_outer_dims()
    x2 = x.flatten_outer_dims()
    o0 = out_0.flatten_outer_dims()
    o1 = out_1.flatten_outer_dims()

    with ExitStack() as ctx:
        const = ctx.enter_context(tc.tile_pool(name="const", bufs=1))
        work = ctx.enter_context(tc.tile_pool(name="work", bufs=2))
        psum = ctx.enter_context(tc.psum_pool(name="psum", bufs=8))

        def wt(shape, dtype, tag, bufs, idx):
            return work.tile(shape, dtype, tag=tag, name="%s_%d" % (tag, idx), bufs=bufs, align_bytes=64)

        cnt = {"bank": 0, "lw": 0, "il": 0, "qw": 0, "gst": 0, "grpa": 0, "phase2": 0}

        def bank():
            cnt["bank"] += 1
            return psum.tile([P, 512], F32, tag="bank", name="bank_%d" % cnt["bank"])

        ident = const.tile([P, P], F32, name="ident")
        neg_half = const.tile([P, 1], F32, name="neg_half")
        warm = const.tile([P, 1], F32, name="warm")
        warm2 = const.tile([P, 1], F32, name="warm2")
        bo_bc = const.tile([P, D], BF16, name="bo_bc")
        nw_bc = const.tile([P, D], BF16, name="nw_bc")
        ident_bf = const.tile([P, P], BF16, name="ident_bf")
        rows = const.tile([P, 2 * CW], BF16, name="rows")
        hc = {}
        hp = {}
        for j in range(NT):
            hc[j] = const.tile([P, NG * P], U32, name="hc_%d" % j, align_bytes=64)
            hp[j] = const.tile([P, P], U8, name="hp_%d" % j, align_bytes=64)

        make_identity(nc, ident[:])
        make_identity(nc, ident_bf[:])
        ctx.enter_context(tc.manual_schedule())

        araw, xraw, xmid, hbf, ac, ap = {}, {}, {}, {}, {}, {}
        ss, ms, rstd, s1acc = {}, {}, {}, {}
        tpa, tph, grpa, grph = {}, {}, {}, {}
        raw, grpw, wc, wp, b1bc = {}, {}, {}, {}, {}

        def load_attn(i):
            if i < NT:
                araw[i] = wt([P, D], BF16, "araw", 2, i)
                nc.sync.dma_start(out=araw[i][:], in_=attn2[i * P : (i + 1) * P, :])

        def load_x(i):
            if i < NT:
                xraw[i] = wt([P, D], BF16, "xraw", 2, i)
                nc.sync.dma_start(out=xraw[i][:], in_=x2[i * P : (i + 1) * P, :])

        def load_b1(q):
            b1bc[q] = wt([P, 2 * CW], BF16, "b1bc", 3, q)
            spread(4 + q, b1bc[q][:], nc.scalar.copy)

        def spread(r, dst, eng_copy):
            cnt["bank"] += 1
            bk = psum.tile([P, 2 * CW], BF16, tag="bank", name="bank_%d" % cnt["bank"])
            for s in range(2):
                nc.tensor.matmul(
                    out=bk[:, s * CW : (s + 1) * CW],
                    lhsT=ident_bf[:, r : r + 1].to_broadcast([P, P]),
                    rhs=rows[:, s * CW : (s + 1) * CW],
                    start=True,
                    stop=True,
                )
            eng_copy(out=dst, in_=bk[:])

        def lw_upto(n):
            while cnt["lw"] < min(n, N_RAW):
                r = cnt["lw"]
                g = r % 4
                if r < N_WO_RAW:
                    mat, pr = wo, r // 4
                    raw[r] = wt([P, 4, 2 * CW], BF16, "wcb", 4, 100 + r)
                else:
                    mat, pr = w1, r // 4 - 2
                    raw[r] = wt([P, 4, 2 * CW], BF16, "wraw", 2, r)
                nc.sync.dma_start(
                    out=raw[r][:],
                    in_=mat[g * 512 : (g + 1) * 512, pr * 2 * CW : (pr + 1) * 2 * CW].rearrange("(p j) c -> p j c", j=4),
                )
                cnt["lw"] += 1

        def il_upto(n):
            while cnt["il"] < min(n, 2 * N_RAW):
                k = cnt["il"]
                grpw[k] = wt([P, 4 * CW], BF16, "grpw", 3, k)
                dst = grpw[k][:].rearrange("p (c j) -> p c j", j=4)
                src = raw[k // 2][:, :, (k % 2) * CW : (k % 2 + 1) * CW].rearrange("p j c -> p c j")
                if k % 2 == 0 and not (16 <= k < 32):
                    nc.vector.tensor_copy(out=dst, in_=src)
                else:
                    nc.scalar.copy(out=dst, in_=src)
                cnt["il"] += 1

        def quant_w(k):
            r = k // 2
            g = r % 4
            cid = 2 * (r // 4) + k % 2
            if g == 0:
                ab = "a" if (cid // 4) % 2 == 0 else "b"
                wc[cid] = wt([P, NG * CW], U32, "wc" + ab, 4, cid)
                wp[cid] = wt([P, CW], U8, "wp" + ab, 4, cid)
            nc.vector.quantize_mx(
                out=wc[cid][:, g * CW : (g + 1) * CW].bitcast(FP8X4),
                scales=wp[cid][4 * g : P, :],
                in_=grpw[k][:],
            )

        def tick_q(n):
            for t in range(n):
                k = cnt["qw"]
                if k < 2 * N_RAW:
                    lw_upto(k // 2 + (RAW_AHEAD_HEAD + 1 if k < 2 * N_WO_RAW - 2 * RAW_AHEAD_HEAD else 3))
                    quant_w(k)
                    cnt["qw"] = k + 1

        def tick_i():
            il_upto(cnt["qw"] + 2)

        def transposes(src, is_sorted):
            words = src[:].bitcast(F32)
            banks = [bank(), bank()]
            for g in range(NG):
                for u in range(2):
                    s = 2 * (g % 2) + u
                    if is_sorted:
                        in_words = words[:, (2 * g + u) * P : (2 * g + u + 1) * P]
                    else:
                        in_words = words[:, 256 * g + u : 256 * (g + 1) : 2]
                    nc.tensor.transpose(out=banks[g // 2][:, s * P : (s + 1) * P], in_=in_words, identity=ident[:])
            return banks

        def copy_out(banks):
            cnt["grpa"] += 1
            grp = wt([P, D], BF16, "grpa", 2, cnt["grpa"])
            for b in range(2):
                nc.scalar.copy(
                    out=grp[:, b * 1024 : (b + 1) * 1024].bitcast(F32).rearrange("p (g r u) -> p g r u", g=2, u=2),
                    in_=banks[b][:].rearrange("p (g u r) -> p g r u", g=2, u=2),
                )
            return grp

        def quant4(grp, codes, plane):
            for g in range(NG):
                nc.vector.quantize_mx(
                    out=codes[:, g * P : (g + 1) * P].bitcast(FP8X4),
                    scales=plane[4 * g : P, :],
                    in_=grp[:, g * 512 : (g + 1) * 512],
                )

        def mm_pass(acc, lc, lp_g, cid, g):
            nc.tensor.matmul_mx(
                out=acc[:],
                lhsT=lc[:, g * P : (g + 1) * P].bitcast(FP8X4),
                lhsT_scale=lp_g,
                rhs=wc[cid][:, g * CW : (g + 1) * CW].bitcast(FP8X4),
                rhs_scale=wp[cid][4 * g : P, :],
                start=(g == 0),
                stop=(g == NG - 1),
            )

        def x_plus_bo(i, pieces):
            if i < NT:
                if i not in xmid:
                    xmid[i] = wt([P, D], F32, "xmid", 2, i)
                for n in pieces:
                    sl = slice(n * 2 * CW, (n + 1) * 2 * CW)
                    eng = nc.gpsimd if n in XB_GPSIMD_PIECES else nc.vector
                    eng.tensor_tensor(out=xmid[i][:, sl], in0=xraw[i][:, sl], in1=bo_bc[:, sl], op=ALU.add)

        def attn_t(i):
            if i < NT:
                tpa[i] = transposes(araw[i], False)

        def attn_c(i):
            if i < NT:
                grpa[i] = copy_out(tpa[i])

        def attn_q(i):
            if i < NT:
                ac[i] = wt([P, NG * P], U32, "ac", 3, i)
                ap[i] = wt([P, NG * P], U8, "ap", 3, i)
                nc.vector.quantize_mx(out=ac[i][:].bitcast(FP8X4), scales=ap[i][:], in_=grpa[i][:])

        def head_extras(t):
            if t == 2:
                load_attn(1)
            if t == 3:
                load_x(1)
                load_attn(2)
            if t == 5:
                attn_t(1)
                attn_c(1)
            if t == 6:
                load_attn(3)
                attn_q(1)
                spread(2, nw_bc[:, 0 : 2 * CW], nc.scalar.copy)
                spread(3, nw_bc[:, 2 * CW : 4 * CW], nc.scalar.copy)

        def mid_slot(i):
            if i >= 2:
                quant4(grph[i - 2], hc[i - 2], hp[i - 2])
            if i >= 1:
                attn_q(i + 1)
            tick_q(prep_in_slot(i))

        def stage1_out(i, pr):
            accs = s1acc[(i, pr)]
            for half in range(2):
                n = 2 * pr + half
                sl = slice(n * CW, (n + 1) * CW)
                nc.vector.tensor_tensor(out=xmid[i][:, sl], in0=accs[half][:], in1=xmid[i][:, sl], op=ALU.add)
            if pr == 1:
                mid_slot(i)
            for half in range(2):
                n = 2 * pr + half
                sl = slice(n * CW, (n + 1) * CW)
                nc.scalar.activation(
                    out=hbf[i][:, sl], in_=xmid[i][:, sl], func=ACT.Square, accum_out=ss[i][:, n : n + 1]
                )

        def stage1(i):
            hbf[i] = wt([P, D], BF16, "hbf", 2, i)
            ss[i] = wt([P, 4], F32, "ss", 2, i)
            for pr in range(2):
                accs = [bank(), bank()]
                if i == 0:
                    for g in range(NG):
                        tick_q(2)
                        tick_i()
                        head_extras(4 * pr + g)
                        for half in range(2):
                            mm_pass(accs[half], ac[i], ap[i][:, g * P : (g + 1) * P], 2 * pr + half, g)
                else:
                    for half in range(2):
                        for g in range(NG):
                            mm_pass(accs[half], ac[i], ap[i][:, g * P : (g + 1) * P], 2 * pr + half, g)
                s1acc[(i, pr)] = accs
                if i > 0:
                    stage1_out(i, pr)
            if i == 0:
                x_plus_bo(0, range(2))
                x_plus_bo(1, range(2))
                load_x(2)
                stage1_out(0, 0)
                stage1_out(0, 1)
            nc.sync.dma_start(out=o0[i * P : (i + 1) * P, :], in_=xmid[i][:])
            junk = wt([P, 4], F32, "junk", 2, i)
            ms[i] = wt([P, 1], F32, "ms", 2, i)
            rstd[i] = wt([P, 1], F32, "rstd", 2, i)
            nc.scalar.activation(
                out=junk[:], in_=ss[i][:], func=ACT.Identity, scale=1.0 / D, bias=EPS / 4.0, accum_out=ms[i][:]
            )
            nc.gpsimd.tensor_tensor(out=rstd[i][:], in0=ms[i][:], in1=neg_half[:], op=ALU.pow)
            x_plus_bo(i + 2, (0, 1))

        def norm(i):
            for g in range(NG):
                gs = slice(g * 512, (g + 1) * 512)
                for u in range(2):
                    nc.vector.scalar_tensor_tensor(
                        out=hbf[i][:, (2 * g + u) * 256 : (2 * g + u + 1) * 256].rearrange("p (m e) -> p m e", e=2),
                        in0=xmid[i][:, gs].rearrange("p (m u e) -> p u m e", u=2, e=2)[:, u, :, :],
                        scalar=rstd[i][:, 0:1],
                        in1=nw_bc[:, gs].rearrange("p (m u e) -> p u m e", u=2, e=2)[:, u, :, :],
                        op0=ALU.mult,
                        op1=ALU.mult,
                    )

        def stage2(q, j):
            accs = [bank(), bank()]
            for half in range(2):
                for g in range(NG):
                    mm_pass(accs[half], hc[j], hp[j][4 * g : P, :], 4 + 2 * q + half, g)
            cnt["gst"] += 1
            tag, bufs = "gst", 4
            if cnt["phase2"] > 0:
                tag, bufs = STAGE_TAGS[cnt["gst"] % len(STAGE_TAGS)]
            gst = wt([P, 2 * CW], F32, tag, bufs, 1000 + cnt["gst"])
            for half in range(2):
                sl = slice(half * CW, (half + 1) * CW)
                nc.vector.tensor_tensor(out=gst[:, sl], in0=accs[half][:], in1=b1bc[q][:, sl], op=ALU.add)
            parts = 2 if (q, j) == (7, NT - 1) else 1
            w = 2 * CW // parts
            for s in range(parts):
                nc.scalar.activation(out=gst[:, s * w : (s + 1) * w], in_=gst[:, s * w : (s + 1) * w], func=ACT.Gelu)
                nc.sync.dma_start(
                    out=o1[j * P : (j + 1) * P, q * 2 * CW + s * w : q * 2 * CW + (s + 1) * w], in_=gst[:, s * w : (s + 1) * w]
                )

        nc.vector.memset(warm[:], 0.0)
        nc.vector.memset(neg_half[:], -0.5)
        nc.scalar.activation(out=warm2[:], in_=warm[:], func=ACT.Gelu)
        nc.vector.memset(rows[:], 0.0)
        load_attn(0)
        nc.sync.dma_start(out=rows[0:2, :], in_=bo.rearrange("(r c) -> r c", c=2 * CW))
        nc.sync.dma_start(out=rows[2:4, :], in_=mlp_norm_w.rearrange("(r c) -> r c", c=2 * CW))
        nc.sync.dma_start(out=rows[4:12, :], in_=b1.rearrange("(r c) -> r c", c=2 * CW))
        lw_upto(RAW_AHEAD_HEAD)
        load_x(0)
        spread(0, bo_bc[:, 0 : 2 * CW], nc.vector.tensor_copy)
        spread(1, bo_bc[:, 2 * CW : 4 * CW], nc.vector.tensor_copy)
        attn_t(0)
        attn_c(0)
        il_upto(2)
        attn_q(0)

        todo = [(q, j) for j in range(NT) for q in range(2)]
        done = set()
        for i in range(NT + 2):
            if i > 0:
                load_attn(i + 3)
                load_x(i + 2)
            if i < NT:
                stage1(i)
            if i == 5:
                load_b1(1)
            if i == 1:
                load_b1(0)
            if i == 20:
                load_b1(2)
            if i >= NT:
                mid_slot(i)
            attn_t(i + 2)
            if 1 <= i <= NT:
                tph[i - 1] = transposes(hbf[i - 1], True)
            attn_c(i + 2)
            if 1 <= i <= NT:
                grph[i - 1] = copy_out(tph[i - 1])
            if i < NT:
                norm(i)
            tick_i()
            left = units_in_slot(i)
            for q, j in todo:
                if left > 0 and (q, j) not in done and j <= i - 2 and i >= PAIR_READY_SLOT[q]:
                    stage2(q, j)
                    done.add((q, j))
                    left -= 1

        cnt["phase2"] = 1
        rest = [u for u in todo if u not in done]
        n0 = len(rest)
        rest.extend([(q, j) for q in range(2, 8) for j in range(NT)])
        tick_at = set([0] + [2 + 6 * t for t in range(20)])
        lb_at = dict([(n0 + 24 * (q - 3) + 1, q) for q in range(3, 8)])
        for idx, (q, j) in enumerate(rest):
            stage2(q, j)
            if idx in tick_at:
                tick_q(2)
                tick_i()
            if idx in lb_at:
                load_b1(lb_at[idx])
